import numpy as np
import ml_dtypes


def mxq(x, axis, fmt="e4m3"):
    dtype, down = {"e4m3": (ml_dtypes.float8_e4m3fn, 7), "e5m2": (ml_dtypes.float8_e5m2, 14)}[fmt]
    v = np.moveaxis(np.asarray(x, np.float32).astype(ml_dtypes.bfloat16).astype(np.float64), axis, -1)
    blocks = v.reshape(v.shape[:-1] + (-1, 32))
    amax = np.abs(blocks).max(-1, keepdims=True)
    byte = np.maximum(np.where(amax > 0, np.frexp(amax)[1] - 1 + 127, 0) - down, 1)
    scale = np.exp2(byte - 127.0)
    codes = (blocks / scale).astype(np.float32).astype(dtype).astype(np.float64)
    return np.moveaxis((codes * scale).reshape(v.shape), -1, axis)


WIDE = False


def mx_kscale(k):
    if not WIDE:
        return np.ones(k)
    levels = np.array([10, -10, 5, -5, 0])
    a = np.random.permutation(np.resize(levels, k // 512 * 4)).reshape(k // 512, 4)
    idx = np.arange(k)
    return np.exp2(a[idx // 512, idx % 128 // 32])


BF16 = ml_dtypes.bfloat16


def bf(x):
    return np.asarray(x, np.float32).astype(BF16)


def f64(x):
    return np.asarray(x).astype(np.float64)


B, N, R = 4096, 1024, 512


def setup_inputs():
    s = np.exp2(np.round(np.log2(mx_kscale(N)) / 2))
    return {"input_state": bf(np.random.standard_normal((B, N)) * s),
            "T": bf(np.random.standard_normal((R, N)) * 0.03 / (s * s)[None, :])}


def reference(input_state, T):
    x = f64(input_state)
    h = x * x
    return mxq(h, 1, "e4m3") @ mxq(f64(T), 1, "e4m3").T

@@ -1,0 +1,235 @@
+from contextlib import ExitStack
+
+import concourse.mybir as mybir
+from concourse.masks import make_identity
+
+F32 = mybir.dt.float32
+BF16 = mybir.dt.bfloat16
+U32 = mybir.dt.uint32
+U8 = mybir.dt.uint8
+FP8X4 = mybir.dt.float8_e4m3fn_x4
+SQUARE = mybir.ActivationFunctionType.Square
+MULT = mybir.AluOpType.mult
+
+P = 128
+B, N, R = 4096, 1024, 512
+FLOPS = 2 * B * N * R
+
+NB = B // P
+NP = NB // 2
+LOOK = 2
+LOADS = (("x", 2), ("t", 0), ("t", 1), ("x", 2), ("x", 2), ("x", 2), ("x", 4), ("x", 4), ("x", 8), ("x", 8))
+ROUTE_D = (1,)
+ROUTE_S = (3, 7, 11, 15, 19, 23, 27, 31)
+ACT_OUT = (28, 29, 31)
+SPLIT_Q = (15,)
+TC_ENGINE = ("A", "D", "A", "A")
+
+
+def tile_custom_final_pooling_2d_kernel(tc, input_state, T, out):
+    nc = tc.nc
+    with ExitStack() as ctx:
+        const = ctx.enter_context(tc.tile_pool(name="const", bufs=1))
+        xin = ctx.enter_context(tc.tile_pool(name="xin", bufs=1))
+        tkeep = ctx.enter_context(tc.tile_pool(name="tkeep", bufs=1))
+        grpp = ctx.enter_context(tc.tile_pool(name="grpp", bufs=4))
+        rawp = ctx.enter_context(tc.tile_pool(name="rawp", bufs=3))
+        codep = ctx.enter_context(tc.tile_pool(name="codep", bufs=3))
+        outp = ctx.enter_context(tc.tile_pool(name="outp", bufs=1))
+        tpp = ctx.enter_context(tc.psum_pool(name="tpp", bufs=4))
+        accp = ctx.enter_context(tc.psum_pool(name="accp", bufs=4))
+        ctx.enter_context(tc.manual_schedule())
+
+        ident = const.tile([P, P], F32, name="ident")
+        make_identity(nc, ident[:])
+
+        x_words = {}
+        o_dram = {}
+        t_words = {}
+        b0 = 0
+        for kind, arg in LOADS:
+            if kind == "t":
+                t_sb = tkeep.tile([P, 4, N // 2], BF16, name="t_sb%d" % arg)
+                nc.sync.dma_start(
+                    out=t_sb[:],
+                    in_=T[:, arg * (N // 2) : (arg + 1) * (N // 2)].rearrange("(a p) n -> p a n", p=P),
+                )
+                t_words[arg] = t_sb[:].bitcast(F32)
+            else:
+                x_sb = xin.tile([P, arg, N], BF16, name="x_sb%d" % b0)
+                rows = slice(b0 * P, (b0 + arg) * P)
+                nc.sync.dma_start(out=x_sb[:], in_=input_state[rows, :].rearrange("(p i) n -> p i n", i=arg))
+                xw = x_sb[:].bitcast(F32)
+                ov = out[rows, :].rearrange("(p i) c -> p i c", i=arg)
+                for i in range(arg):
+                    x_words[b0 + i] = xw[:, i, :]
+                    o_dram[b0 + i] = (ov, i)
+                b0 += arg
+
+        tp_of = {}
+        grp_of = {}
+        raw_of = {}
+        code_of = {}
+        acc_of = {}
+        o_of = {}
+        tbank = {}
+        tgrp = {}
+        tcode = {}
+
+        def transposes(k):
+            for b in (2 * k, 2 * k + 1):
+                tp = tpp.tile([P, 512], F32, name="tp%d" % b, tag="tp")
+                for q in range(4):
+                    nc.tensor.transpose(tp[:, q * P : (q + 1) * P], x_words[b][:, q * P : (q + 1) * P], ident[:])
+                tp_of[b] = tp
+
+        def grouped(k):
+            if k not in grp_of:
+                grp_of[k] = grpp.tile([P, 2 * N], BF16, name="grp%d" % k, tag="grp", align_bytes=64)
+            return grp_of[k]
+
+        def copy_words(b, engine):
+            raw = rawp.tile([P, N], BF16, name="raw%d" % b, tag="raw", align_bytes=64)
+            dst = raw[:].bitcast(F32).rearrange("p (g r u) -> p g r u", g=2, u=2)
+            src = tp_of[b][:].rearrange("p (g u r) -> p g r u", g=2, u=2)
+            if engine == "A":
+                nc.scalar.copy(out=dst, in_=src)
+            else:
+                nc.vector.tensor_copy(out=dst, in_=src)
+            raw_of[b] = raw
+
+        def multiply(b):
+            g = grouped(b // 2)
+            nc.vector.tensor_tensor(
+                out=g[:, (b % 2) * N : (b % 2 + 1) * N], in0=raw_of[b][:], in1=raw_of[b][:], op=MULT
+            )
+
+        def square_scalar(k):
+            for b in (2 * k, 2 * k + 1):
+                if b in ROUTE_D:
+                    continue
+                if b in ROUTE_S:
+                    copy_words(b, "A")
+                    continue
+                g = grouped(k)
+                bank = tp_of[b][:].bitcast(BF16)
+                for h in range(2):
+                    nc.scalar.activation(
+                        out=g[:, (b % 2) * N + h * 512 : (b % 2) * N + (h + 1) * 512].rearrange(
+                            "p (r u e) -> p r u e", u=2, e=2
+                        ),
+                        in_=bank[:, h * 512 : (h + 1) * 512].rearrange("p (u r e) -> p r u e", u=2, e=2),
+                        func=SQUARE,
+                    )
+
+        def square_vector(k):
+            for b in (2 * k, 2 * k + 1):
+                if b in ROUTE_D:
+                    copy_words(b, "D")
+                    multiply(b)
+
+        def quantise(k):
+            codes = codep.tile([P, 512], U32, name="codes%d" % k, tag="codes", align_bytes=64)
+            scales = codep.tile([P, 512], U8, name="scales%d" % k, tag="scales", align_bytes=64)
+            code_of[k] = (codes, scales)
+            g = grouped(k)
+            if k in SPLIT_Q:
+                for i in range(2):
+                    if 2 * k + i in ROUTE_S:
+                        multiply(2 * k + i)
+                    nc.vector.quantize_mx(
+                        out=codes[:, i * 256 : (i + 1) * 256].bitcast(FP8X4),
+                        scales=scales[:, i * 256 : (i + 1) * 256],
+                        in_=g[:, i * N : (i + 1) * N],
+                    )
+            else:
+                for i in range(2):
+                    if 2 * k + i in ROUTE_S:
+                        multiply(2 * k + i)
+                nc.vector.quantize_mx(out=codes[:].bitcast(FP8X4), scales=scales[:], in_=g[:])
+
+        def passes(k):
+            codes, scales = code_of[k]
+            for i in range(2):
+                acc = accp.tile([P, R], F32, name="acc%d" % (2 * k + i), tag="acc")
+                for h in range(2):
+                    cols = slice((2 * i + h) * P, (2 * i + h + 1) * P)
+                    nc.tensor.matmul_mx(
+                        out=acc[:],
+                        lhsT=codes[:, cols].bitcast(FP8X4),
+                        lhsT_scale=scales[:, cols],
+                        rhs=tcode[h][0][:].bitcast(FP8X4),
+                        rhs_scale=tcode[h][1][:],
+                        start=(h == 0),
+                        stop=(h == 1),
+                    )
+                acc_of[2 * k + i] = acc
+
+        def copy_out(k):
+            o_sb = outp.tile([P, 2, R], F32, name="o_sb%d" % k)
+            for i in range(2):
+                b = 2 * k + i
+                if b in ACT_OUT:
+                    nc.scalar.copy(out=o_sb[:, i, :], in_=acc_of[b][:])
+                else:
+                    nc.vector.tensor_copy(out=o_sb[:, i, :], in_=acc_of[b][:])
+            ov, i0 = o_dram[2 * k]
+            nc.sync.dma_start(out=ov[:, i0 : i0 + 2, :], in_=o_sb[:])
+
+        def t_transposes(h):
+            for j in range(2):
+                bank = accp.tile([P, 512], F32, name="tbank%d" % (2 * h + j), tag="acc")
+                for aa in range(2):
+                    for u in range(2):
+                        nc.tensor.transpose(
+                            bank[:, (2 * aa + u) * P : (2 * aa + u + 1) * P],
+                            t_words[h][:, 2 * j + aa, u * P : (u + 1) * P],
+                            ident[:],
+                        )
+                tbank[2 * h + j] = bank
+
+        def t_copy(n):
+            h, j = n // 2, n % 2
+            if h not in tgrp:
+                tgrp[h] = tkeep.tile([P, 4 * R], BF16, name="tgrp%d" % h, align_bytes=64)
+            dst = tgrp[h][:].bitcast(F32)[:, j * 512 : (j + 1) * 512].rearrange("p (a r u) -> p a r u", a=2, u=2)
+            src = tbank[n][:].rearrange("p (a u r) -> p a r u", a=2, u=2)
+            if TC_ENGINE[n] == "A":
+                nc.scalar.copy(out=dst, in_=src)
+            else:
+                nc.vector.tensor_copy(out=dst, in_=src)
+
+        def t_quantise(h):
+            codes = tkeep.tile([P, R], U32, name="tcodes%d" % h, align_bytes=64)
+            scales = tkeep.tile([P, R], U8, name="tscales%d" % h, align_bytes=64)
+            nc.vector.quantize_mx(out=codes[:].bitcast(FP8X4), scales=scales[:], in_=tgrp[h][:])
+            tcode[h] = (codes, scales)
+
+        transposes(0)
+        square_scalar(0)
+        square_vector(0)
+        t_transposes(0)
+        t_copy(0)
+        t_copy(1)
+        t_transposes(1)
+        t_quantise(0)
+        t_copy(2)
+        t_copy(3)
+        t_quantise(1)
+        transposes(1)
+        square_scalar(1)
+        square_vector(1)
+
+        for k in range(NP + 1):
+            if k + LOOK < NP:
+                transposes(k + LOOK)
+            if k < NP:
+                quantise(k)
+            if k + LOOK < NP:
+                square_scalar(k + LOOK)
+            if k >= 1:
+                copy_out(k - 1)
+            if k < NP:
+                passes(k)
+            if k + LOOK < NP:
+                square_vector(k + LOOK)

@@ -18,12 +18,25 @@ FLOPS = 2 * B * N * R
 NB = B // P
 NP = NB // 2
 LOOK = 2
-LOADS = (("x", 2), ("t", 0), ("t", 1), ("x", 2), ("x", 2), ("x", 2), ("x", 4), ("x", 4), ("x", 8), ("x", 8))
+LOADS = (
+    ("x", 2),
+    ("t", 0),
+    ("t", 1),
+    ("t", 2),
+    ("t", 3),
+    ("x", 2),
+    ("x", 2),
+    ("x", 2),
+    ("x", 4),
+    ("x", 4),
+    ("x", 8),
+    ("x", 8),
+)
 ROUTE_D = (1,)
 ROUTE_S = (3, 7, 11, 15, 19, 23, 27, 31)
 ACT_OUT = (28, 29, 31)
-SPLIT_Q = (15,)
-TC_ENGINE = ("A", "D", "A", "A")
+SPLIT = (15,)
+TC_ENGINE = ("A", "D", "A", "D")
 
 
 def tile_custom_final_pooling_2d_kernel(tc, input_state, T, out):
@@ -49,10 +62,11 @@ def tile_custom_final_pooling_2d_kernel(tc, input_state, T, out):
         b0 = 0
         for kind, arg in LOADS:
             if kind == "t":
-                t_sb = tkeep.tile([P, 4, N // 2], BF16, name="t_sb%d" % arg)
+                h, j = arg // 2, arg % 2
+                t_sb = tkeep.tile([P, 2, N // 2], BF16, name="t_sb%d" % arg)
                 nc.sync.dma_start(
                     out=t_sb[:],
-                    in_=T[:, arg * (N // 2) : (arg + 1) * (N // 2)].rearrange("(a p) n -> p a n", p=P),
+                    in_=T[j * 256 : (j + 1) * 256, h * 512 : (h + 1) * 512].rearrange("(a p) n -> p a n", p=P),
                 )
                 t_words[arg] = t_sb[:].bitcast(F32)
             else:
@@ -71,7 +85,6 @@ def tile_custom_final_pooling_2d_kernel(tc, input_state, T, out):
         raw_of = {}
         code_of = {}
         acc_of = {}
-        o_of = {}
         tbank = {}
         tgrp = {}
         tcode = {}
@@ -79,8 +92,13 @@ def tile_custom_final_pooling_2d_kernel(tc, input_state, T, out):
         def transposes(k):
             for b in (2 * k, 2 * k + 1):
                 tp = tpp.tile([P, 512], F32, name="tp%d" % b, tag="tp")
-                for q in range(4):
-                    nc.tensor.transpose(tp[:, q * P : (q + 1) * P], x_words[b][:, q * P : (q + 1) * P], ident[:])
+                for g in range(2):
+                    for u in range(2):
+                        nc.tensor.transpose(
+                            tp[:, (2 * u + g) * P : (2 * u + g + 1) * P],
+                            x_words[b][:, (2 * g + u) * P : (2 * g + u + 1) * P],
+                            ident[:],
+                        )
                 tp_of[b] = tp
 
         def grouped(k):
@@ -88,14 +106,17 @@ def tile_custom_final_pooling_2d_kernel(tc, input_state, T, out):
                 grp_of[k] = grpp.tile([P, 2 * N], BF16, name="grp%d" % k, tag="grp", align_bytes=64)
             return grp_of[k]
 
-        def copy_words(b, engine):
-            raw = rawp.tile([P, N], BF16, name="raw%d" % b, tag="raw", align_bytes=64)
-            dst = raw[:].bitcast(F32).rearrange("p (g r u) -> p g r u", g=2, u=2)
-            src = tp_of[b][:].rearrange("p (g u r) -> p g r u", g=2, u=2)
+        def interleave(dst_words, bank, engine):
+            dst = dst_words.rearrange("p (r u) -> p r u", u=2)
+            src = bank[:].rearrange("p (u r) -> p r u", u=2)
             if engine == "A":
                 nc.scalar.copy(out=dst, in_=src)
             else:
                 nc.vector.tensor_copy(out=dst, in_=src)
+
+        def copy_words(b, engine):
+            raw = rawp.tile([P, N], BF16, name="raw%d" % b, tag="raw", align_bytes=64)
+            interleave(raw[:].bitcast(F32), tp_of[b], engine)
             raw_of[b] = raw
 
         def multiply(b):
@@ -112,15 +133,11 @@ def tile_custom_final_pooling_2d_kernel(tc, input_state, T, out):
                     copy_words(b, "A")
                     continue
                 g = grouped(k)
-                bank = tp_of[b][:].bitcast(BF16)
-                for h in range(2):
-                    nc.scalar.activation(
-                        out=g[:, (b % 2) * N + h * 512 : (b % 2) * N + (h + 1) * 512].rearrange(
-                            "p (r u e) -> p r u e", u=2, e=2
-                        ),
-                        in_=bank[:, h * 512 : (h + 1) * 512].rearrange("p (u r e) -> p r u e", u=2, e=2),
-                        func=SQUARE,
-                    )
+                nc.scalar.activation(
+                    out=g[:, (b % 2) * N : (b % 2 + 1) * N].rearrange("p (r u e) -> p r u e", u=2, e=2),
+                    in_=tp_of[b][:].bitcast(BF16).rearrange("p (u r e) -> p r u e", u=2, e=2),
+                    func=SQUARE,
+                )
 
         def square_vector(k):
             for b in (2 * k, 2 * k + 1):
@@ -133,7 +150,7 @@ def tile_custom_final_pooling_2d_kernel(tc, input_state, T, out):
             scales = codep.tile([P, 512], U8, name="scales%d" % k, tag="scales", align_bytes=64)
             code_of[k] = (codes, scales)
             g = grouped(k)
-            if k in SPLIT_Q:
+            if k in SPLIT:
                 for i in range(2):
                     if 2 * k + i in ROUTE_S:
                         multiply(2 * k + i)
@@ -167,55 +184,49 @@ def tile_custom_final_pooling_2d_kernel(tc, input_state, T, out):
 
         def copy_out(k):
             o_sb = outp.tile([P, 2, R], F32, name="o_sb%d" % k)
+            ov, i0 = o_dram[2 * k]
             for i in range(2):
                 b = 2 * k + i
                 if b in ACT_OUT:
                     nc.scalar.copy(out=o_sb[:, i, :], in_=acc_of[b][:])
                 else:
                     nc.vector.tensor_copy(out=o_sb[:, i, :], in_=acc_of[b][:])
-            ov, i0 = o_dram[2 * k]
-            nc.sync.dma_start(out=ov[:, i0 : i0 + 2, :], in_=o_sb[:])
+                if k in SPLIT:
+                    nc.sync.dma_start(out=ov[:, i0 + i, :], in_=o_sb[:, i, :])
+            if k not in SPLIT:
+                nc.sync.dma_start(out=ov[:, i0 : i0 + 2, :], in_=o_sb[:])
 
-        def t_transposes(h):
-            for j in range(2):
-                bank = accp.tile([P, 512], F32, name="tbank%d" % (2 * h + j), tag="acc")
-                for aa in range(2):
-                    for u in range(2):
-                        nc.tensor.transpose(
-                            bank[:, (2 * aa + u) * P : (2 * aa + u + 1) * P],
-                            t_words[h][:, 2 * j + aa, u * P : (u + 1) * P],
-                            ident[:],
-                        )
-                tbank[2 * h + j] = bank
-
-        def t_copy(n):
+        def t_quarter(n):
             h, j = n // 2, n % 2
+            bank = accp.tile([P, 512], F32, name="tbank%d" % n, tag="acc")
+            for a in range(2):
+                for u in range(2):
+                    nc.tensor.transpose(
+                        bank[:, (2 * u + a) * P : (2 * u + a + 1) * P],
+                        t_words[n][:, a, u * P : (u + 1) * P],
+                        ident[:],
+                    )
             if h not in tgrp:
                 tgrp[h] = tkeep.tile([P, 4 * R], BF16, name="tgrp%d" % h, align_bytes=64)
-            dst = tgrp[h][:].bitcast(F32)[:, j * 512 : (j + 1) * 512].rearrange("p (a r u) -> p a r u", a=2, u=2)
-            src = tbank[n][:].rearrange("p (a u r) -> p a r u", a=2, u=2)
-            if TC_ENGINE[n] == "A":
-                nc.scalar.copy(out=dst, in_=src)
-            else:
-                nc.vector.tensor_copy(out=dst, in_=src)
-
-        def t_quantise(h):
-            codes = tkeep.tile([P, R], U32, name="tcodes%d" % h, align_bytes=64)
-            scales = tkeep.tile([P, R], U8, name="tscales%d" % h, align_bytes=64)
-            nc.vector.quantize_mx(out=codes[:].bitcast(FP8X4), scales=scales[:], in_=tgrp[h][:])
-            tcode[h] = (codes, scales)
+                tcode[h] = (
+                    tkeep.tile([P, R], U32, name="tcodes%d" % h, align_bytes=64),
+                    tkeep.tile([P, R], U8, name="tscales%d" % h, align_bytes=64),
+                )
+            interleave(tgrp[h][:].bitcast(F32)[:, j * 512 : (j + 1) * 512], bank, TC_ENGINE[n])
+            nc.vector.quantize_mx(
+                out=tcode[h][0][:, j * 256 : (j + 1) * 256].bitcast(FP8X4),
+                scales=tcode[h][1][:, j * 256 : (j + 1) * 256],
+                in_=tgrp[h][:, j * 1024 : (j + 1) * 1024],
+            )
 
         transposes(0)
         square_scalar(0)
         square_vector(0)
-        t_transposes(0)
-        t_copy(0)
-        t_copy(1)
-        t_transposes(1)
-        t_quantise(0)
-        t_copy(2)
-        t_copy(3)
-        t_quantise(1)
+        t_quarter(0)
+        t_quarter(1)
+        quantise(0)
+        t_quarter(2)
+        t_quarter(3)
         transposes(1)
         square_scalar(1)
         square_vector(1)
@@ -223,7 +234,7 @@ def tile_custom_final_pooling_2d_kernel(tc, input_state, T, out):
         for k in range(NP + 1):
             if k + LOOK < NP:
                 transposes(k + LOOK)
-            if k < NP:
+            if 1 <= k < NP:
                 quantise(k)
             if k + LOOK < NP:
                 square_scalar(k + LOOK)

@@ -19,7 +19,8 @@ NB = B // P
 NP = NB // 2
 LOOK = 2
 LOADS = (
-    ("x", 2),
+    ("x", 1),
+    ("x", 1),
     ("t", 0),
     ("t", 1),
     ("t", 2),
@@ -35,8 +36,10 @@ LOADS = (
 ROUTE_D = (1,)
 ROUTE_S = (3, 7, 11, 15, 19, 23, 27, 31)
 ACT_OUT = (28, 29, 31)
-SPLIT = (15,)
+SPLIT_Q = (15,)
+SPLIT_STORE = (0, 15)
 TC_ENGINE = ("A", "D", "A", "D")
+PRE_WARM = 6
 
 
 def tile_custom_final_pooling_2d_kernel(tc, input_state, T, out):
@@ -53,6 +56,8 @@ def tile_custom_final_pooling_2d_kernel(tc, input_state, T, out):
         accp = ctx.enter_context(tc.psum_pool(name="accp", bufs=4))
         ctx.enter_context(tc.manual_schedule())
 
+        zeros = const.tile([P, 512], BF16, name="zeros")
+        nc.vector.memset(zeros[:], 0.0)
         ident = const.tile([P, P], F32, name="ident")
         make_identity(nc, ident[:])
 
@@ -62,12 +67,8 @@ def tile_custom_final_pooling_2d_kernel(tc, input_state, T, out):
         b0 = 0
         for kind, arg in LOADS:
             if kind == "t":
-                h, j = arg // 2, arg % 2
-                t_sb = tkeep.tile([P, 2, N // 2], BF16, name="t_sb%d" % arg)
-                nc.sync.dma_start(
-                    out=t_sb[:],
-                    in_=T[j * 256 : (j + 1) * 256, h * 512 : (h + 1) * 512].rearrange("(a p) n -> p a n", p=P),
-                )
+                t_sb = tkeep.tile([P, N], BF16, name="t_sb%d" % arg)
+                nc.sync.dma_start(out=t_sb[:], in_=T[arg * P : (arg + 1) * P, :])
                 t_words[arg] = t_sb[:].bitcast(F32)
             else:
                 x_sb = xin.tile([P, arg, N], BF16, name="x_sb%d" % b0)
@@ -85,38 +86,48 @@ def tile_custom_final_pooling_2d_kernel(tc, input_state, T, out):
         raw_of = {}
         code_of = {}
         acc_of = {}
-        tbank = {}
-        tgrp = {}
-        tcode = {}
+        warm_of = {}
 
-        def transposes(k):
+        tgrp = tkeep.tile([P, 2, 4 * R], BF16, name="tgrp", align_bytes=64)
+        tcodes = tkeep.tile([P, 2, R], U32, name="tcodes", align_bytes=64)
+        tscales = tkeep.tile([P, 2, R], U8, name="tscales", align_bytes=64)
+
+        def new_warm_bank(n):
+            warm_of[0] = accp.tile([P, 512], F32, name="warm%d" % n, tag="acc")
+
+        def warm(n):
+            for i in range(n):
+                nc.tensor.matmul(out=warm_of[0][:], lhsT=zeros[:, 0:P], rhs=zeros[:], start=True, stop=True)
+
+        def four_transposes(bank, words):
+            for g in range(2):
+                for u in range(2):
+                    nc.tensor.transpose(
+                        bank[:, (2 * u + g) * P : (2 * u + g + 1) * P],
+                        words[:, (2 * g + u) * P : (2 * g + u + 1) * P],
+                        ident[:],
+                    )
+
+        def transposes(k, warm_after=0):
             for b in (2 * k, 2 * k + 1):
                 tp = tpp.tile([P, 512], F32, name="tp%d" % b, tag="tp")
-                for g in range(2):
-                    for u in range(2):
-                        nc.tensor.transpose(
-                            tp[:, (2 * u + g) * P : (2 * u + g + 1) * P],
-                            x_words[b][:, (2 * g + u) * P : (2 * g + u + 1) * P],
-                            ident[:],
-                        )
+                four_transposes(tp, x_words[b])
                 tp_of[b] = tp
+                warm(warm_after)
 
         def grouped(k):
             if k not in grp_of:
                 grp_of[k] = grpp.tile([P, 2 * N], BF16, name="grp%d" % k, tag="grp", align_bytes=64)
             return grp_of[k]
 
-        def interleave(dst_words, bank, engine):
-            dst = dst_words.rearrange("p (r u) -> p r u", u=2)
-            src = bank[:].rearrange("p (u r) -> p r u", u=2)
+        def copy_words(b, engine):
+            raw = rawp.tile([P, N], BF16, name="raw%d" % b, tag="raw", align_bytes=64)
+            dst = raw[:].bitcast(F32).rearrange("p (r u) -> p r u", u=2)
+            src = tp_of[b][:].rearrange("p (u r) -> p r u", u=2)
             if engine == "A":
                 nc.scalar.copy(out=dst, in_=src)
             else:
                 nc.vector.tensor_copy(out=dst, in_=src)
-
-        def copy_words(b, engine):
-            raw = rawp.tile([P, N], BF16, name="raw%d" % b, tag="raw", align_bytes=64)
-            interleave(raw[:].bitcast(F32), tp_of[b], engine)
             raw_of[b] = raw
 
         def multiply(b):
@@ -150,7 +161,7 @@ def tile_custom_final_pooling_2d_kernel(tc, input_state, T, out):
             scales = codep.tile([P, 512], U8, name="scales%d" % k, tag="scales", align_bytes=64)
             code_of[k] = (codes, scales)
             g = grouped(k)
-            if k in SPLIT:
+            if k in SPLIT_Q:
                 for i in range(2):
                     if 2 * k + i in ROUTE_S:
                         multiply(2 * k + i)
@@ -175,8 +186,8 @@ def tile_custom_final_pooling_2d_kernel(tc, input_state, T, out):
                         out=acc[:],
                         lhsT=codes[:, cols].bitcast(FP8X4),
                         lhsT_scale=scales[:, cols],
-                        rhs=tcode[h][0][:].bitcast(FP8X4),
-                        rhs_scale=tcode[h][1][:],
+                        rhs=tcodes[:, h, :].bitcast(FP8X4),
+                        rhs_scale=tscales[:, h, :],
                         start=(h == 0),
                         stop=(h == 1),
                     )
@@ -184,50 +195,52 @@ def tile_custom_final_pooling_2d_kernel(tc, input_state, T, out):
 
         def copy_out(k):
             o_sb = outp.tile([P, 2, R], F32, name="o_sb%d" % k)
-            ov, i0 = o_dram[2 * k]
             for i in range(2):
                 b = 2 * k + i
                 if b in ACT_OUT:
                     nc.scalar.copy(out=o_sb[:, i, :], in_=acc_of[b][:])
                 else:
                     nc.vector.tensor_copy(out=o_sb[:, i, :], in_=acc_of[b][:])
-                if k in SPLIT:
-                    nc.sync.dma_start(out=ov[:, i0 + i, :], in_=o_sb[:, i, :])
-            if k not in SPLIT:
+                if k in SPLIT_STORE:
+                    ov, i0 = o_dram[b]
+                    nc.sync.dma_start(out=ov[:, i0, :], in_=o_sb[:, i, :])
+            if k not in SPLIT_STORE:
+                ov, i0 = o_dram[2 * k]
                 nc.sync.dma_start(out=ov[:, i0 : i0 + 2, :], in_=o_sb[:])
 
-        def t_quarter(n):
-            h, j = n // 2, n % 2
-            bank = accp.tile([P, 512], F32, name="tbank%d" % n, tag="acc")
-            for a in range(2):
-                for u in range(2):
-                    nc.tensor.transpose(
-                        bank[:, (2 * u + a) * P : (2 * u + a + 1) * P],
-                        t_words[n][:, a, u * P : (u + 1) * P],
-                        ident[:],
-                    )
-            if h not in tgrp:
-                tgrp[h] = tkeep.tile([P, 4 * R], BF16, name="tgrp%d" % h, align_bytes=64)
-                tcode[h] = (
-                    tkeep.tile([P, R], U32, name="tcodes%d" % h, align_bytes=64),
-                    tkeep.tile([P, R], U8, name="tscales%d" % h, align_bytes=64),
+        def t_block(a):
+            bank = accp.tile([P, 512], F32, name="tbank%d" % a, tag="acc")
+            four_transposes(bank, t_words[a])
+            dst = tgrp[:].bitcast(F32)[:, :, a * 256 : (a + 1) * 256].rearrange("p h (r u) -> p h r u", u=2)
+            src = bank[:].rearrange("p (u h r) -> p h r u", u=2, h=2)
+            if TC_ENGINE[a] == "A":
+                nc.scalar.copy(out=dst, in_=src)
+            else:
+                nc.vector.tensor_copy(out=dst, in_=src)
+            for h in range(2):
+                nc.vector.quantize_mx(
+                    out=tcodes[:, h, a * P : (a + 1) * P].bitcast(FP8X4),
+                    scales=tscales[:, h, a * P : (a + 1) * P],
+                    in_=tgrp[:, h, a * 512 : (a + 1) * 512],
                 )
-            interleave(tgrp[h][:].bitcast(F32)[:, j * 512 : (j + 1) * 512], bank, TC_ENGINE[n])
-            nc.vector.quantize_mx(
-                out=tcode[h][0][:, j * 256 : (j + 1) * 256].bitcast(FP8X4),
-                scales=tcode[h][1][:, j * 256 : (j + 1) * 256],
-                in_=tgrp[h][:, j * 1024 : (j + 1) * 1024],
-            )
 
-        transposes(0)
+        new_warm_bank(0)
+        warm(PRE_WARM)
+        transposes(0, warm_after=1)
         square_scalar(0)
         square_vector(0)
-        t_quarter(0)
-        t_quarter(1)
+        t_block(0)
+        warm(1)
+        t_block(1)
+        warm(1)
         quantise(0)
-        t_quarter(2)
-        t_quarter(3)
+        t_block(2)
+        warm(1)
+        t_block(3)
+        new_warm_bank(1)
+        warm(2)
         transposes(1)
+        warm(1)
         square_scalar(1)
         square_vector(1)
 

@@ -18,9 +18,9 @@ FLOPS = 2 * B * N * R
 NB = B // P
 NP = NB // 2
 LOOK = 2
+LONG_FROM = 2
 LOADS = (
-    ("x", 1),
-    ("x", 1),
+    ("x", 2),
     ("t", 0),
     ("t", 1),
     ("t", 2),
@@ -36,10 +36,8 @@ LOADS = (
 ROUTE_D = (1,)
 ROUTE_S = (3, 7, 11, 15, 19, 23, 27, 31)
 ACT_OUT = (28, 29, 31)
-SPLIT_Q = (15,)
-SPLIT_STORE = (0, 15)
+SPLIT = (15,)
 TC_ENGINE = ("A", "D", "A", "D")
-PRE_WARM = 6
 
 
 def tile_custom_final_pooling_2d_kernel(tc, input_state, T, out):
@@ -56,8 +54,6 @@ def tile_custom_final_pooling_2d_kernel(tc, input_state, T, out):
         accp = ctx.enter_context(tc.psum_pool(name="accp", bufs=4))
         ctx.enter_context(tc.manual_schedule())
 
-        zeros = const.tile([P, 512], BF16, name="zeros")
-        nc.vector.memset(zeros[:], 0.0)
         ident = const.tile([P, P], F32, name="ident")
         make_identity(nc, ident[:])
 
@@ -67,8 +63,12 @@ def tile_custom_final_pooling_2d_kernel(tc, input_state, T, out):
         b0 = 0
         for kind, arg in LOADS:
             if kind == "t":
-                t_sb = tkeep.tile([P, N], BF16, name="t_sb%d" % arg)
-                nc.sync.dma_start(out=t_sb[:], in_=T[arg * P : (arg + 1) * P, :])
+                h, j = arg // 2, arg % 2
+                t_sb = tkeep.tile([P, 2, N // 2], BF16, name="t_sb%d" % arg)
+                nc.sync.dma_start(
+                    out=t_sb[:],
+                    in_=T[j * 256 : (j + 1) * 256, h * 512 : (h + 1) * 512].rearrange("(a p) n -> p a n", p=P),
+                )
                 t_words[arg] = t_sb[:].bitcast(F32)
             else:
                 x_sb = xin.tile([P, arg, N], BF16, name="x_sb%d" % b0)
@@ -86,48 +86,38 @@ def tile_custom_final_pooling_2d_kernel(tc, input_state, T, out):
         raw_of = {}
         code_of = {}
         acc_of = {}
-        warm_of = {}
+        tbank = {}
+        tgrp = {}
+        tcode = {}
 
-        tgrp = tkeep.tile([P, 2, 4 * R], BF16, name="tgrp", align_bytes=64)
-        tcodes = tkeep.tile([P, 2, R], U32, name="tcodes", align_bytes=64)
-        tscales = tkeep.tile([P, 2, R], U8, name="tscales", align_bytes=64)
-
-        def new_warm_bank(n):
-            warm_of[0] = accp.tile([P, 512], F32, name="warm%d" % n, tag="acc")
-
-        def warm(n):
-            for i in range(n):
-                nc.tensor.matmul(out=warm_of[0][:], lhsT=zeros[:, 0:P], rhs=zeros[:], start=True, stop=True)
-
-        def four_transposes(bank, words):
-            for g in range(2):
-                for u in range(2):
-                    nc.tensor.transpose(
-                        bank[:, (2 * u + g) * P : (2 * u + g + 1) * P],
-                        words[:, (2 * g + u) * P : (2 * g + u + 1) * P],
-                        ident[:],
-                    )
-
-        def transposes(k, warm_after=0):
+        def transposes(k):
             for b in (2 * k, 2 * k + 1):
                 tp = tpp.tile([P, 512], F32, name="tp%d" % b, tag="tp")
-                four_transposes(tp, x_words[b])
+                for g in range(2):
+                    for u in range(2):
+                        nc.tensor.transpose(
+                            tp[:, (2 * u + g) * P : (2 * u + g + 1) * P],
+                            x_words[b][:, (2 * g + u) * P : (2 * g + u + 1) * P],
+                            ident[:],
+                        )
                 tp_of[b] = tp
-                warm(warm_after)
 
         def grouped(k):
             if k not in grp_of:
                 grp_of[k] = grpp.tile([P, 2 * N], BF16, name="grp%d" % k, tag="grp", align_bytes=64)
             return grp_of[k]
 
-        def copy_words(b, engine):
-            raw = rawp.tile([P, N], BF16, name="raw%d" % b, tag="raw", align_bytes=64)
-            dst = raw[:].bitcast(F32).rearrange("p (r u) -> p r u", u=2)
-            src = tp_of[b][:].rearrange("p (u r) -> p r u", u=2)
+        def interleave(dst_words, bank, engine):
+            dst = dst_words.rearrange("p (r u) -> p r u", u=2)
+            src = bank[:].rearrange("p (u r) -> p r u", u=2)
             if engine == "A":
                 nc.scalar.copy(out=dst, in_=src)
             else:
                 nc.vector.tensor_copy(out=dst, in_=src)
+
+        def copy_words(b, engine):
+            raw = rawp.tile([P, N], BF16, name="raw%d" % b, tag="raw", align_bytes=64)
+            interleave(raw[:].bitcast(F32), tp_of[b], engine)
             raw_of[b] = raw
 
         def multiply(b):
@@ -161,7 +151,7 @@ def tile_custom_final_pooling_2d_kernel(tc, input_state, T, out):
             scales = codep.tile([P, 512], U8, name="scales%d" % k, tag="scales", align_bytes=64)
             code_of[k] = (codes, scales)
             g = grouped(k)
-            if k in SPLIT_Q:
+            if k in SPLIT:
                 for i in range(2):
                     if 2 * k + i in ROUTE_S:
                         multiply(2 * k + i)
@@ -186,8 +176,8 @@ def tile_custom_final_pooling_2d_kernel(tc, input_state, T, out):
                         out=acc[:],
                         lhsT=codes[:, cols].bitcast(FP8X4),
                         lhsT_scale=scales[:, cols],
-                        rhs=tcodes[:, h, :].bitcast(FP8X4),
-                        rhs_scale=tscales[:, h, :],
+                        rhs=tcode[h][0][:].bitcast(FP8X4),
+                        rhs_scale=tcode[h][1][:],
                         start=(h == 0),
                         stop=(h == 1),
                     )
@@ -195,65 +185,73 @@ def tile_custom_final_pooling_2d_kernel(tc, input_state, T, out):
 
         def copy_out(k):
             o_sb = outp.tile([P, 2, R], F32, name="o_sb%d" % k)
+            ov, i0 = o_dram[2 * k]
             for i in range(2):
                 b = 2 * k + i
                 if b in ACT_OUT:
                     nc.scalar.copy(out=o_sb[:, i, :], in_=acc_of[b][:])
                 else:
                     nc.vector.tensor_copy(out=o_sb[:, i, :], in_=acc_of[b][:])
-                if k in SPLIT_STORE:
-                    ov, i0 = o_dram[b]
-                    nc.sync.dma_start(out=ov[:, i0, :], in_=o_sb[:, i, :])
-            if k not in SPLIT_STORE:
-                ov, i0 = o_dram[2 * k]
+                if k in SPLIT:
+                    nc.sync.dma_start(out=ov[:, i0 + i, :], in_=o_sb[:, i, :])
+            if k not in SPLIT:
                 nc.sync.dma_start(out=ov[:, i0 : i0 + 2, :], in_=o_sb[:])
 
-        def t_block(a):
-            bank = accp.tile([P, 512], F32, name="tbank%d" % a, tag="acc")
-            four_transposes(bank, t_words[a])
-            dst = tgrp[:].bitcast(F32)[:, :, a * 256 : (a + 1) * 256].rearrange("p h (r u) -> p h r u", u=2)
-            src = bank[:].rearrange("p (u h r) -> p h r u", u=2, h=2)
-            if TC_ENGINE[a] == "A":
-                nc.scalar.copy(out=dst, in_=src)
-            else:
-                nc.vector.tensor_copy(out=dst, in_=src)
-            for h in range(2):
-                nc.vector.quantize_mx(
-                    out=tcodes[:, h, a * P : (a + 1) * P].bitcast(FP8X4),
-                    scales=tscales[:, h, a * P : (a + 1) * P],
-                    in_=tgrp[:, h, a * 512 : (a + 1) * 512],
+        def t_quarter(n):
+            h, j = n // 2, n % 2
+            bank = accp.tile([P, 512], F32, name="tbank%d" % n, tag="acc")
+            for a in range(2):
+                for u in range(2):
+                    nc.tensor.transpose(
+                        bank[:, (2 * u + a) * P : (2 * u + a + 1) * P],
+                        t_words[n][:, a, u * P : (u + 1) * P],
+                        ident[:],
+                    )
+            if h not in tgrp:
+                tgrp[h] = tkeep.tile([P, 4 * R], BF16, name="tgrp%d" % h, align_bytes=64)
+                tcode[h] = (
+                    tkeep.tile([P, R], U32, name="tcodes%d" % h, align_bytes=64),
+                    tkeep.tile([P, R], U8, name="tscales%d" % h, align_bytes=64),
                 )
+            interleave(tgrp[h][:].bitcast(F32)[:, j * 512 : (j + 1) * 512], bank, TC_ENGINE[n])
+            nc.vector.quantize_mx(
+                out=tcode[h][0][:, j * 256 : (j + 1) * 256].bitcast(FP8X4),
+                scales=tcode[h][1][:, j * 256 : (j + 1) * 256],
+                in_=tgrp[h][:, j * 1024 : (j + 1) * 1024],
+            )
 
-        new_warm_bank(0)
-        warm(PRE_WARM)
-        transposes(0, warm_after=1)
+        transposes(0)
         square_scalar(0)
         square_vector(0)
-        t_block(0)
-        warm(1)
-        t_block(1)
-        warm(1)
+        t_quarter(0)
+        t_quarter(1)
         quantise(0)
-        t_block(2)
-        warm(1)
-        t_block(3)
-        new_warm_bank(1)
-        warm(2)
+        t_quarter(2)
+        t_quarter(3)
         transposes(1)
-        warm(1)
         square_scalar(1)
         square_vector(1)
 
         for k in range(NP + 1):
-            if k + LOOK < NP:
+            long_runs = k >= LONG_FROM
+            first_of_two = (k - LONG_FROM) % 2 == 0
+            if not long_runs:
                 transposes(k + LOOK)
+            elif first_of_two:
+                for q in (k + LOOK, k + LOOK + 1):
+                    if q < NP:
+                        transposes(q)
             if 1 <= k < NP:
                 quantise(k)
             if k + LOOK < NP:
                 square_scalar(k + LOOK)
+            if k < NP:
+                if not long_runs:
+                    passes(k)
+                elif not first_of_two:
+                    passes(k - 1)
+                    passes(k)
             if k >= 1:
                 copy_out(k - 1)
-            if k < NP:
-                passes(k)
             if k + LOOK < NP:
                 square_vector(k + LOOK)

@@ -8,7 +8,6 @@ BF16 = mybir.dt.bfloat16
 U32 = mybir.dt.uint32
 U8 = mybir.dt.uint8
 FP8X4 = mybir.dt.float8_e4m3fn_x4
-SQUARE = mybir.ActivationFunctionType.Square
 MULT = mybir.AluOpType.mult
 
 P = 128
@@ -17,8 +16,7 @@ FLOPS = 2 * B * N * R
 
 NB = B // P
 NP = NB // 2
-LOOK = 2
-LONG_FROM = 2
+LOOK = 3
 LOADS = (
     ("x", 2),
     ("t", 0),
@@ -33,11 +31,8 @@ LOADS = (
     ("x", 8),
     ("x", 8),
 )
-ROUTE_D = (1,)
-ROUTE_S = (3, 7, 11, 15, 19, 23, 27, 31)
-ACT_OUT = (28, 29, 31)
-SPLIT = (15,)
-TC_ENGINE = ("A", "D", "A", "D")
+VECTOR_OUT = (4, 10, 14, 20, 24, 30)
+LAST = NP - 1
 
 
 def tile_custom_final_pooling_2d_kernel(tc, input_state, T, out):
@@ -46,8 +41,8 @@ def tile_custom_final_pooling_2d_kernel(tc, input_state, T, out):
         const = ctx.enter_context(tc.tile_pool(name="const", bufs=1))
         xin = ctx.enter_context(tc.tile_pool(name="xin", bufs=1))
         tkeep = ctx.enter_context(tc.tile_pool(name="tkeep", bufs=1))
-        grpp = ctx.enter_context(tc.tile_pool(name="grpp", bufs=4))
         rawp = ctx.enter_context(tc.tile_pool(name="rawp", bufs=3))
+        grpp = ctx.enter_context(tc.tile_pool(name="grpp", bufs=4))
         codep = ctx.enter_context(tc.tile_pool(name="codep", bufs=3))
         outp = ctx.enter_context(tc.tile_pool(name="outp", bufs=1))
         tpp = ctx.enter_context(tc.psum_pool(name="tpp", bufs=4))
@@ -82,8 +77,8 @@ def tile_custom_final_pooling_2d_kernel(tc, input_state, T, out):
                 b0 += arg
 
         tp_of = {}
-        grp_of = {}
         raw_of = {}
+        grp_of = {}
         code_of = {}
         acc_of = {}
         tbank = {}
@@ -102,68 +97,41 @@ def tile_custom_final_pooling_2d_kernel(tc, input_state, T, out):
                         )
                 tp_of[b] = tp
 
-        def grouped(k):
-            if k not in grp_of:
-                grp_of[k] = grpp.tile([P, 2 * N], BF16, name="grp%d" % k, tag="grp", align_bytes=64)
-            return grp_of[k]
-
-        def interleave(dst_words, bank, engine):
-            dst = dst_words.rearrange("p (r u) -> p r u", u=2)
-            src = bank[:].rearrange("p (u r) -> p r u", u=2)
-            if engine == "A":
-                nc.scalar.copy(out=dst, in_=src)
-            else:
-                nc.vector.tensor_copy(out=dst, in_=src)
-
-        def copy_words(b, engine):
-            raw = rawp.tile([P, N], BF16, name="raw%d" % b, tag="raw", align_bytes=64)
-            interleave(raw[:].bitcast(F32), tp_of[b], engine)
-            raw_of[b] = raw
-
-        def multiply(b):
-            g = grouped(b // 2)
-            nc.vector.tensor_tensor(
-                out=g[:, (b % 2) * N : (b % 2 + 1) * N], in0=raw_of[b][:], in1=raw_of[b][:], op=MULT
+        def interleave(dst_words, bank):
+            nc.scalar.copy(
+                out=dst_words.rearrange("p (r u) -> p r u", u=2), in_=bank[:].rearrange("p (u r) -> p r u", u=2)
             )
 
-        def square_scalar(k):
-            for b in (2 * k, 2 * k + 1):
-                if b in ROUTE_D:
-                    continue
-                if b in ROUTE_S:
-                    copy_words(b, "A")
-                    continue
-                g = grouped(k)
-                nc.scalar.activation(
-                    out=g[:, (b % 2) * N : (b % 2 + 1) * N].rearrange("p (r u e) -> p r u e", u=2, e=2),
-                    in_=tp_of[b][:].bitcast(BF16).rearrange("p (u r e) -> p r u e", u=2, e=2),
-                    func=SQUARE,
-                )
+        def copy_words(k):
+            raw = rawp.tile([P, 2 * N], BF16, name="raw%d" % k, tag="raw", align_bytes=64)
+            for i in range(2):
+                interleave(raw[:].bitcast(F32)[:, i * 512 : (i + 1) * 512], tp_of[2 * k + i])
+            raw_of[k] = raw
 
-        def square_vector(k):
-            for b in (2 * k, 2 * k + 1):
-                if b in ROUTE_D:
-                    copy_words(b, "D")
-                    multiply(b)
+        def multiply(k):
+            grp = grpp.tile([P, 2 * N], BF16, name="grp%d" % k, tag="grp", align_bytes=64)
+            raw = raw_of[k]
+            if k == LAST:
+                for i in range(2):
+                    cols = slice(i * N, (i + 1) * N)
+                    nc.vector.tensor_tensor(out=grp[:, cols], in0=raw[:, cols], in1=raw[:, cols], op=MULT)
+            else:
+                nc.vector.tensor_tensor(out=grp[:], in0=raw[:], in1=raw[:], op=MULT)
+            grp_of[k] = grp
 
         def quantise(k):
             codes = codep.tile([P, 512], U32, name="codes%d" % k, tag="codes", align_bytes=64)
             scales = codep.tile([P, 512], U8, name="scales%d" % k, tag="scales", align_bytes=64)
             code_of[k] = (codes, scales)
-            g = grouped(k)
-            if k in SPLIT:
+            g = grp_of[k]
+            if k == LAST:
                 for i in range(2):
-                    if 2 * k + i in ROUTE_S:
-                        multiply(2 * k + i)
                     nc.vector.quantize_mx(
                         out=codes[:, i * 256 : (i + 1) * 256].bitcast(FP8X4),
                         scales=scales[:, i * 256 : (i + 1) * 256],
                         in_=g[:, i * N : (i + 1) * N],
                     )
             else:
-                for i in range(2):
-                    if 2 * k + i in ROUTE_S:
-                        multiply(2 * k + i)
                 nc.vector.quantize_mx(out=codes[:].bitcast(FP8X4), scales=scales[:], in_=g[:])
 
         def passes(k):
@@ -188,13 +156,13 @@ def tile_custom_final_pooling_2d_kernel(tc, input_state, T, out):
             ov, i0 = o_dram[2 * k]
             for i in range(2):
                 b = 2 * k + i
-                if b in ACT_OUT:
-                    nc.scalar.copy(out=o_sb[:, i, :], in_=acc_of[b][:])
-                else:
+                if b in VECTOR_OUT:
                     nc.vector.tensor_copy(out=o_sb[:, i, :], in_=acc_of[b][:])
-                if k in SPLIT:
+                else:
+                    nc.scalar.copy(out=o_sb[:, i, :], in_=acc_of[b][:])
+                if k == LAST:
                     nc.sync.dma_start(out=ov[:, i0 + i, :], in_=o_sb[:, i, :])
-            if k not in SPLIT:
+            if k != LAST:
                 nc.sync.dma_start(out=ov[:, i0 : i0 + 2, :], in_=o_sb[:])
 
         def t_quarter(n):
@@ -213,7 +181,10 @@ def tile_custom_final_pooling_2d_kernel(tc, input_state, T, out):
                     tkeep.tile([P, R], U32, name="tcodes%d" % h, align_bytes=64),
                     tkeep.tile([P, R], U8, name="tscales%d" % h, align_bytes=64),
                 )
-            interleave(tgrp[h][:].bitcast(F32)[:, j * 512 : (j + 1) * 512], bank, TC_ENGINE[n])
+            interleave(tgrp[h][:].bitcast(F32)[:, j * 512 : (j + 1) * 512], bank)
+
+        def t_quantise(n):
+            h, j = n // 2, n % 2
             nc.vector.quantize_mx(
                 out=tcode[h][0][:, j * 256 : (j + 1) * 256].bitcast(FP8X4),
                 scales=tcode[h][1][:, j * 256 : (j + 1) * 256],
@@ -221,37 +192,32 @@ def tile_custom_final_pooling_2d_kernel(tc, input_state, T, out):
             )
 
         transposes(0)
-        square_scalar(0)
-        square_vector(0)
+        copy_words(0)
         t_quarter(0)
         t_quarter(1)
-        quantise(0)
+        multiply(0)
+        t_quantise(0)
+        t_quantise(1)
         t_quarter(2)
         t_quarter(3)
+        quantise(0)
+        t_quantise(2)
+        t_quantise(3)
         transposes(1)
-        square_scalar(1)
-        square_vector(1)
+        copy_words(1)
+        multiply(1)
+        transposes(2)
+        copy_words(2)
 
         for k in range(NP + 1):
-            long_runs = k >= LONG_FROM
-            first_of_two = (k - LONG_FROM) % 2 == 0
-            if not long_runs:
+            if k + LOOK < NP:
                 transposes(k + LOOK)
-            elif first_of_two:
-                for q in (k + LOOK, k + LOOK + 1):
-                    if q < NP:
-                        transposes(q)
+                copy_words(k + LOOK)
             if 1 <= k < NP:
                 quantise(k)
-            if k + LOOK < NP:
-                square_scalar(k + LOOK)
             if k < NP:
-                if not long_runs:
-                    passes(k)
-                elif not first_of_two:
-                    passes(k - 1)
-                    passes(k)
+                passes(k)
             if k >= 1:
                 copy_out(k - 1)
-            if k + LOOK < NP:
-                square_vector(k + LOOK)
+            if k + LOOK - 1 < NP:
+                multiply(k + LOOK - 1)

@@ -31,6 +31,7 @@ LOADS = (
     ("x", 8),
     ("x", 8),
 )
+STORES = (8, 8, 4, 4, 2, 2, 2, 1, 1)
 VECTOR_OUT = (4, 10, 14, 20, 24, 30)
 LAST = NP - 1
 
@@ -52,60 +53,65 @@ def tile_custom_final_pooling_2d_kernel(tc, input_state, T, out):
         ident = const.tile([P, P], F32, name="ident")
         make_identity(nc, ident[:])
 
+        x_view = input_state.rearrange("(p i) n -> p i n", i=NB)
+        o_view = out.rearrange("(p i) c -> p i c", i=NB)
+
         x_words = {}
-        o_dram = {}
         t_words = {}
         b0 = 0
         for kind, arg in LOADS:
             if kind == "t":
-                h, j = arg // 2, arg % 2
-                t_sb = tkeep.tile([P, 2, N // 2], BF16, name="t_sb%d" % arg)
-                nc.sync.dma_start(
-                    out=t_sb[:],
-                    in_=T[j * 256 : (j + 1) * 256, h * 512 : (h + 1) * 512].rearrange("(a p) n -> p a n", p=P),
-                )
+                t_sb = tkeep.tile([P, N], BF16, name="t_sb%d" % arg)
+                nc.sync.dma_start(out=t_sb[:], in_=T[arg * P : (arg + 1) * P, :])
                 t_words[arg] = t_sb[:].bitcast(F32)
             else:
                 x_sb = xin.tile([P, arg, N], BF16, name="x_sb%d" % b0)
-                rows = slice(b0 * P, (b0 + arg) * P)
-                nc.sync.dma_start(out=x_sb[:], in_=input_state[rows, :].rearrange("(p i) n -> p i n", i=arg))
+                nc.sync.dma_start(out=x_sb[:], in_=x_view[:, b0 : b0 + arg, :])
                 xw = x_sb[:].bitcast(F32)
-                ov = out[rows, :].rearrange("(p i) c -> p i c", i=arg)
                 for i in range(arg):
                     x_words[b0 + i] = xw[:, i, :]
-                    o_dram[b0 + i] = (ov, i)
                 b0 += arg
+
+        unit_of = {}
+        b0 = 0
+        for n in STORES:
+            for i in range(n):
+                unit_of[b0 + i] = (b0, n)
+            b0 += n
 
         tp_of = {}
         raw_of = {}
         grp_of = {}
         code_of = {}
         acc_of = {}
-        tbank = {}
-        tgrp = {}
-        tcode = {}
+        o_of = {}
+
+        tgrp = tkeep.tile([P, 2, 4 * R], BF16, name="tgrp", align_bytes=64)
+        tcodes = tkeep.tile([P, 2, R], U32, name="tcodes", align_bytes=64)
+        tscales = tkeep.tile([P, 2, R], U8, name="tscales", align_bytes=64)
+
+        def four_transposes(bank, words):
+            for g in range(2):
+                for u in range(2):
+                    nc.tensor.transpose(
+                        bank[:, (2 * u + g) * P : (2 * u + g + 1) * P],
+                        words[:, (2 * g + u) * P : (2 * g + u + 1) * P],
+                        ident[:],
+                    )
 
         def transposes(k):
             for b in (2 * k, 2 * k + 1):
                 tp = tpp.tile([P, 512], F32, name="tp%d" % b, tag="tp")
-                for g in range(2):
-                    for u in range(2):
-                        nc.tensor.transpose(
-                            tp[:, (2 * u + g) * P : (2 * u + g + 1) * P],
-                            x_words[b][:, (2 * g + u) * P : (2 * g + u + 1) * P],
-                            ident[:],
-                        )
+                four_transposes(tp, x_words[b])
                 tp_of[b] = tp
-
-        def interleave(dst_words, bank):
-            nc.scalar.copy(
-                out=dst_words.rearrange("p (r u) -> p r u", u=2), in_=bank[:].rearrange("p (u r) -> p r u", u=2)
-            )
 
         def copy_words(k):
             raw = rawp.tile([P, 2 * N], BF16, name="raw%d" % k, tag="raw", align_bytes=64)
             for i in range(2):
-                interleave(raw[:].bitcast(F32)[:, i * 512 : (i + 1) * 512], tp_of[2 * k + i])
+                nc.scalar.copy(
+                    out=raw[:].bitcast(F32)[:, i * 512 : (i + 1) * 512].rearrange("p (r u) -> p r u", u=2),
+                    in_=tp_of[2 * k + i][:].rearrange("p (u r) -> p r u", u=2),
+                )
             raw_of[k] = raw
 
         def multiply(k):
@@ -144,62 +150,51 @@ def tile_custom_final_pooling_2d_kernel(tc, input_state, T, out):
                         out=acc[:],
                         lhsT=codes[:, cols].bitcast(FP8X4),
                         lhsT_scale=scales[:, cols],
-                        rhs=tcode[h][0][:].bitcast(FP8X4),
-                        rhs_scale=tcode[h][1][:],
+                        rhs=tcodes[:, h, :].bitcast(FP8X4),
+                        rhs_scale=tscales[:, h, :],
                         start=(h == 0),
                         stop=(h == 1),
                     )
                 acc_of[2 * k + i] = acc
 
         def copy_out(k):
-            o_sb = outp.tile([P, 2, R], F32, name="o_sb%d" % k)
-            ov, i0 = o_dram[2 * k]
-            for i in range(2):
-                b = 2 * k + i
+            for b in (2 * k, 2 * k + 1):
+                first, n = unit_of[b]
+                if b == first:
+                    o_of[first] = outp.tile([P, n, R], F32, name="o_sb%d" % first)
+                o_sb = o_of[first]
                 if b in VECTOR_OUT:
-                    nc.vector.tensor_copy(out=o_sb[:, i, :], in_=acc_of[b][:])
+                    nc.vector.tensor_copy(out=o_sb[:, b - first, :], in_=acc_of[b][:])
                 else:
-                    nc.scalar.copy(out=o_sb[:, i, :], in_=acc_of[b][:])
-                if k == LAST:
-                    nc.sync.dma_start(out=ov[:, i0 + i, :], in_=o_sb[:, i, :])
-            if k != LAST:
-                nc.sync.dma_start(out=ov[:, i0 : i0 + 2, :], in_=o_sb[:])
+                    nc.scalar.copy(out=o_sb[:, b - first, :], in_=acc_of[b][:])
+                if b == first + n - 1:
+                    nc.sync.dma_start(out=o_view[:, first : first + n, :], in_=o_sb[:])
 
-        def t_quarter(n):
-            h, j = n // 2, n % 2
-            bank = accp.tile([P, 512], F32, name="tbank%d" % n, tag="acc")
-            for a in range(2):
-                for u in range(2):
-                    nc.tensor.transpose(
-                        bank[:, (2 * u + a) * P : (2 * u + a + 1) * P],
-                        t_words[n][:, a, u * P : (u + 1) * P],
-                        ident[:],
-                    )
-            if h not in tgrp:
-                tgrp[h] = tkeep.tile([P, 4 * R], BF16, name="tgrp%d" % h, align_bytes=64)
-                tcode[h] = (
-                    tkeep.tile([P, R], U32, name="tcodes%d" % h, align_bytes=64),
-                    tkeep.tile([P, R], U8, name="tscales%d" % h, align_bytes=64),
-                )
-            interleave(tgrp[h][:].bitcast(F32)[:, j * 512 : (j + 1) * 512], bank)
-
-        def t_quantise(n):
-            h, j = n // 2, n % 2
-            nc.vector.quantize_mx(
-                out=tcode[h][0][:, j * 256 : (j + 1) * 256].bitcast(FP8X4),
-                scales=tcode[h][1][:, j * 256 : (j + 1) * 256],
-                in_=tgrp[h][:, j * 1024 : (j + 1) * 1024],
+        def t_block(a):
+            bank = accp.tile([P, 512], F32, name="tbank%d" % a, tag="acc")
+            four_transposes(bank, t_words[a])
+            nc.scalar.copy(
+                out=tgrp[:].bitcast(F32)[:, :, a * 256 : (a + 1) * 256].rearrange("p h (r u) -> p h r u", u=2),
+                in_=bank[:].rearrange("p (u h r) -> p h r u", u=2, h=2),
             )
+
+        def t_quantise(a):
+            for h in range(2):
+                nc.vector.quantize_mx(
+                    out=tcodes[:, h, a * P : (a + 1) * P].bitcast(FP8X4),
+                    scales=tscales[:, h, a * P : (a + 1) * P],
+                    in_=tgrp[:, h, a * 512 : (a + 1) * 512],
+                )
 
         transposes(0)
         copy_words(0)
-        t_quarter(0)
-        t_quarter(1)
+        t_block(0)
+        t_block(1)
         multiply(0)
         t_quantise(0)
         t_quantise(1)
-        t_quarter(2)
-        t_quarter(3)
+        t_block(2)
+        t_block(3)
         quantise(0)
         t_quantise(2)
         t_quantise(3)

from contextlib import ExitStack

import concourse.mybir as mybir
from concourse.masks import make_identity

F32 = mybir.dt.float32
BF16 = mybir.dt.bfloat16
U32 = mybir.dt.uint32
U8 = mybir.dt.uint8
FP8X4 = mybir.dt.float8_e4m3fn_x4
MULT = mybir.AluOpType.mult

P = 128
B, N, R = 4096, 1024, 512
FLOPS = 2 * B * N * R

NB = B // P
NP = NB // 2
LOOK = 3
LOADS = (
    ("x", 2),
    ("t", 0),
    ("t", 1),
    ("t", 2),
    ("t", 3),
    ("x", 2),
    ("x", 2),
    ("x", 2),
    ("x", 4),
    ("x", 4),
    ("x", 8),
    ("x", 8),
)
STORES = (8, 8, 4, 4, 2, 2, 2, 1, 1)
VECTOR_OUT = (4, 10, 14, 20, 24, 30)
LAST = NP - 1


def tile_custom_final_pooling_2d_kernel(tc, input_state, T, out):
    nc = tc.nc
    with ExitStack() as ctx:
        const = ctx.enter_context(tc.tile_pool(name="const", bufs=1))
        xin = ctx.enter_context(tc.tile_pool(name="xin", bufs=1))
        tkeep = ctx.enter_context(tc.tile_pool(name="tkeep", bufs=1))
        rawp = ctx.enter_context(tc.tile_pool(name="rawp", bufs=3))
        grpp = ctx.enter_context(tc.tile_pool(name="grpp", bufs=4))
        codep = ctx.enter_context(tc.tile_pool(name="codep", bufs=3))
        outp = ctx.enter_context(tc.tile_pool(name="outp", bufs=1))
        tpp = ctx.enter_context(tc.psum_pool(name="tpp", bufs=4))
        accp = ctx.enter_context(tc.psum_pool(name="accp", bufs=4))
        ctx.enter_context(tc.manual_schedule())

        ident = const.tile([P, P], F32, name="ident")
        make_identity(nc, ident[:])

        x_view = input_state.rearrange("(p i) n -> p i n", i=NB)
        o_view = out.rearrange("(p i) c -> p i c", i=NB)

        x_words = {}
        t_words = {}
        b0 = 0
        for kind, arg in LOADS:
            if kind == "t":
                t_sb = tkeep.tile([P, N], BF16, name="t_sb%d" % arg)
                nc.sync.dma_start(out=t_sb[:], in_=T[arg * P : (arg + 1) * P, :])
                t_words[arg] = t_sb[:].bitcast(F32)
            else:
                x_sb = xin.tile([P, arg, N], BF16, name="x_sb%d" % b0)
                nc.sync.dma_start(out=x_sb[:], in_=x_view[:, b0 : b0 + arg, :])
                xw = x_sb[:].bitcast(F32)
                for i in range(arg):
                    x_words[b0 + i] = xw[:, i, :]
                b0 += arg

        unit_of = {}
        b0 = 0
        for n in STORES:
            for i in range(n):
                unit_of[b0 + i] = (b0, n)
            b0 += n

        tp_of = {}
        raw_of = {}
        grp_of = {}
        code_of = {}
        acc_of = {}
        o_of = {}

        tgrp = tkeep.tile([P, 2, 4 * R], BF16, name="tgrp", align_bytes=64)
        tcodes = tkeep.tile([P, 2, R], U32, name="tcodes", align_bytes=64)
        tscales = tkeep.tile([P, 2, R], U8, name="tscales", align_bytes=64)

        def four_transposes(bank, words):
            for g in range(2):
                for u in range(2):
                    nc.tensor.transpose(
                        bank[:, (2 * u + g) * P : (2 * u + g + 1) * P],
                        words[:, (2 * g + u) * P : (2 * g + u + 1) * P],
                        ident[:],
                    )

        def transposes(k):
            for b in (2 * k, 2 * k + 1):
                tp = tpp.tile([P, 512], F32, name="tp%d" % b, tag="tp")
                four_transposes(tp, x_words[b])
                tp_of[b] = tp

        def copy_words(k):
            raw = rawp.tile([P, 2 * N], BF16, name="raw%d" % k, tag="raw", align_bytes=64)
            for i in range(2):
                nc.scalar.copy(
                    out=raw[:].bitcast(F32)[:, i * 512 : (i + 1) * 512].rearrange("p (r u) -> p r u", u=2),
                    in_=tp_of[2 * k + i][:].rearrange("p (u r) -> p r u", u=2),
                )
            raw_of[k] = raw

        def multiply(k):
            grp = grpp.tile([P, 2 * N], BF16, name="grp%d" % k, tag="grp", align_bytes=64)
            raw = raw_of[k]
            if k == LAST:
                for i in range(2):
                    cols = slice(i * N, (i + 1) * N)
                    nc.vector.tensor_tensor(out=grp[:, cols], in0=raw[:, cols], in1=raw[:, cols], op=MULT)
            else:
                nc.vector.tensor_tensor(out=grp[:], in0=raw[:], in1=raw[:], op=MULT)
            grp_of[k] = grp

        def quantise(k):
            codes = codep.tile([P, 512], U32, name="codes%d" % k, tag="codes", align_bytes=64)
            scales = codep.tile([P, 512], U8, name="scales%d" % k, tag="scales", align_bytes=64)
            code_of[k] = (codes, scales)
            g = grp_of[k]
            if k == LAST:
                for i in range(2):
                    nc.vector.quantize_mx(
                        out=codes[:, i * 256 : (i + 1) * 256].bitcast(FP8X4),
                        scales=scales[:, i * 256 : (i + 1) * 256],
                        in_=g[:, i * N : (i + 1) * N],
                    )
            else:
                nc.vector.quantize_mx(out=codes[:].bitcast(FP8X4), scales=scales[:], in_=g[:])

        def passes(k):
            codes, scales = code_of[k]
            for i in range(2):
                acc = accp.tile([P, R], F32, name="acc%d" % (2 * k + i), tag="acc")
                for h in range(2):
                    cols = slice((2 * i + h) * P, (2 * i + h + 1) * P)
                    nc.tensor.matmul_mx(
                        out=acc[:],
                        lhsT=codes[:, cols].bitcast(FP8X4),
                        lhsT_scale=scales[:, cols],
                        rhs=tcodes[:, h, :].bitcast(FP8X4),
                        rhs_scale=tscales[:, h, :],
                        start=(h == 0),
                        stop=(h == 1),
                    )
                acc_of[2 * k + i] = acc

        def copy_out(k):
            for b in (2 * k, 2 * k + 1):
                first, n = unit_of[b]
                if b == first:
                    o_of[first] = outp.tile([P, n, R], F32, name="o_sb%d" % first)
                o_sb = o_of[first]
                if b in VECTOR_OUT:
                    nc.vector.tensor_copy(out=o_sb[:, b - first, :], in_=acc_of[b][:])
                else:
                    nc.scalar.copy(out=o_sb[:, b - first, :], in_=acc_of[b][:])
                if b == first + n - 1:
                    nc.sync.dma_start(out=o_view[:, first : first + n, :], in_=o_sb[:])

        def t_block(a):
            bank = accp.tile([P, 512], F32, name="tbank%d" % a, tag="acc")
            four_transposes(bank, t_words[a])
            nc.scalar.copy(
                out=tgrp[:].bitcast(F32)[:, :, a * 256 : (a + 1) * 256].rearrange("p h (r u) -> p h r u", u=2),
                in_=bank[:].rearrange("p (u h r) -> p h r u", u=2, h=2),
            )

        def t_quantise(a):
            for h in range(2):
                nc.vector.quantize_mx(
                    out=tcodes[:, h, a * P : (a + 1) * P].bitcast(FP8X4),
                    scales=tscales[:, h, a * P : (a + 1) * P],
                    in_=tgrp[:, h, a * 512 : (a + 1) * 512],
                )

        transposes(0)
        copy_words(0)
        t_block(0)
        t_block(1)
        multiply(0)
        t_quantise(0)
        t_quantise(1)
        t_block(2)
        t_block(3)
        quantise(0)
        t_quantise(2)
        t_quantise(3)
        transposes(1)
        copy_words(1)
        multiply(1)
        transposes(2)
        copy_words(2)

        for k in range(NP + 1):
            if k + LOOK < NP:
                transposes(k + LOOK)
                copy_words(k + LOOK)
            if 1 <= k < NP:
                quantise(k)
            if k < NP:
                passes(k)
            if k >= 1:
                copy_out(k - 1)
            if k + LOOK - 1 < NP:
                multiply(k + LOOK - 1)
